import numpy as np
import ml_dtypes


def mxq(x, axis, fmt="e4m3"):
    dtype, down = {"e4m3": (ml_dtypes.float8_e4m3fn, 7), "e5m2": (ml_dtypes.float8_e5m2, 14)}[fmt]
    v = np.moveaxis(np.asarray(x, np.float32).astype(ml_dtypes.bfloat16).astype(np.float64), axis, -1)
    blocks = v.reshape(v.shape[:-1] + (-1, 32))
    amax = np.abs(blocks).max(-1, keepdims=True)
    byte = np.maximum(np.where(amax > 0, np.frexp(amax)[1] - 1 + 127, 0) - down, 1)
    scale = np.exp2(byte - 127.0)
    codes = (blocks / scale).astype(np.float32).astype(dtype).astype(np.float64)
    return np.moveaxis((codes * scale).reshape(v.shape), -1, axis)


WIDE = False


def mx_kscale(k):
    if not WIDE:
        return np.ones(k)
    levels = np.array([10, -10, 5, -5, 0])
    a = np.random.permutation(np.resize(levels, k // 512 * 4)).reshape(k // 512, 4)
    idx = np.arange(k)
    return np.exp2(a[idx // 512, idx % 128 // 32])


BF16 = ml_dtypes.bfloat16


def bf(x):
    return np.asarray(x, np.float32).astype(BF16)


def f64(x):
    return np.asarray(x).astype(np.float64)


N, C, T, V, S, INTER = 4, 1024, 32, 128, 4, 32
KT = INTER * T


def setup_inputs():
    s = mx_kscale(C)
    u = mx_kscale(KT)[::T]
    g = np.sqrt(1.5) * KT ** 0.25 / np.sqrt(C)
    mu = 0.25 * np.random.standard_normal((1, C, 1, 1))
    return {'x': bf((np.random.standard_normal((N, C, T, V)) + mu) * s[None, :, None, None]),
            'A': bf(2.0 * np.random.random((S, V, V)) / V),
            'PA': bf(np.random.standard_normal((S, V, V)) / V),
            'Wa': bf(np.random.standard_normal((S, INTER, C)) * g * u[None, :, None] / s[None, None, :]),
            'Wb': bf(np.random.standard_normal((S, INTER, C)) * g / u[None, :, None] / s[None, None, :])}


def reference(x, A, PA, Wa, Wb):
    xq = mxq(f64(x).reshape(N, C, T * V), 1, 'e4m3')
    fa = (mxq(f64(Wa).reshape(S * INTER, C), 1, 'e4m3') @ xq).reshape(N, S, KT, V)
    fb = (mxq(f64(Wb).reshape(S * INTER, C), 1, 'e4m3') @ xq).reshape(N, S, KT, V)
    scores = (np.swapaxes(mxq(fa, 2, 'e4m3'), -1, -2) @ mxq(fb, 2, 'e4m3')) / KT
    e = np.exp(scores - scores.max(-2, keepdims=True))
    attn = e / e.sum(-2, keepdims=True)
    return attn + (f64(A) + f64(PA))[None]

@@ -1,0 +1,321 @@
+from contextlib import ExitStack
+
+import concourse.mybir as mybir
+from concourse.masks import make_identity
+
+F32 = mybir.dt.float32
+BF16 = mybir.dt.bfloat16
+U32 = mybir.dt.uint32
+U8 = mybir.dt.uint8
+FP8X4 = mybir.dt.float8_e4m3fn_x4
+ALU = mybir.AluOpType
+ACT = mybir.ActivationFunctionType
+
+N, C, T, V, S, INTER = 4, 1024, 32, 128, 4, 32
+KT = INTER * T
+
+P = 128
+PACK = 4
+K_PASS = P * PACK
+C_PASSES = C // K_PASS
+
+SIDES = 2
+W_ROWS = SIDES * S * INTER
+OPERANDS = SIDES * S
+MATES = INTER // PACK
+
+GROUPS = KT // K_PASS
+ALL_GROUPS = N * GROUPS
+GROUP_FRAMES = T // GROUPS
+GROUP_COLS = GROUP_FRAMES * V
+CHUNKS = ALL_GROUPS * C_PASSES
+HALF_COLS = GROUP_COLS // 2
+SCALAR_COLS = 640
+VECTOR_COLS = GROUP_COLS - SCALAR_COLS
+LOADS_AHEAD = 2
+
+BANK_FRAMES = 2
+GROUP_BANKS = GROUP_FRAMES // BANK_FRAMES
+HALF_BANKS = GROUP_BANKS // 2
+BANK_OPERANDS = 2
+
+FLOPS = 2 * W_ROWS * C * N * T * V + 2 * N * S * V * V * KT
+
+
+def quantise_weights(nc, consts, psum_flip, ident, Wa, Wb):
+    w_rows = consts.tile([P, SIDES * C], BF16)
+    nc.sync.dma_start(out=w_rows[:, 0:C], in_=Wa.rearrange("s i c -> (s i) c"))
+    nc.sync.dma_start(out=w_rows[:, C : 2 * C], in_=Wb.rearrange("s i c -> (s i) c"))
+    w_words = w_rows[:].bitcast(F32)
+    pair_words = C // 2
+
+    w_grouped = consts.tile([P, C_PASSES * W_ROWS * PACK], BF16, align_bytes=64)
+    w_grouped_words = w_grouped[:].bitcast(F32).rearrange(
+        "p (h a q l j u) -> p h a u q l j", h=C_PASSES, a=SIDES, q=S * 2, l=4, j=PACK, u=2
+    )
+    for h in range(C_PASSES):
+        w_flipped = psum_flip.tile([P, SIDES, 2, P], F32, tag="flipped")
+        for a in range(SIDES):
+            for u in range(2):
+                first = a * pair_words + h * (K_PASS // 2) + u
+                nc.tensor.transpose(
+                    w_flipped[:, a, u, :], w_words[:, first : first + K_PASS // 2 - 1 : 2], ident[:]
+                )
+        for a in range(SIDES):
+            for u in range(2):
+                nc.vector.tensor_copy(
+                    out=w_grouped_words[:, h, a, u],
+                    in_=w_flipped[:, a, u, :].rearrange("p (q j l) -> p q l j", q=S * 2, j=PACK, l=4),
+                )
+    w_codes = consts.tile([P, C_PASSES, W_ROWS], U32, align_bytes=64)
+    w_scales = consts.tile([P, C_PASSES, W_ROWS], U8, align_bytes=64)
+    nc.vector.quantize_mx(
+        out=w_codes[:].rearrange("p h r -> p (h r)").bitcast(FP8X4),
+        scales=w_scales[:].rearrange("p h r -> p (h r)"),
+        in_=w_grouped[:],
+    )
+    return w_codes, w_scales
+
+
+def tile_unitagcn_pa_t_kernel(tc, x, A, PA, Wa, Wb, out):
+    nc = tc.nc
+    with ExitStack() as stack:
+        consts = stack.enter_context(tc.tile_pool(name="consts", bufs=1))
+        raw_pool = stack.enter_context(tc.tile_pool(name="raw", bufs=LOADS_AHEAD + 1))
+        grouped_pool = stack.enter_context(tc.tile_pool(name="grouped", bufs=3))
+        xq_pool = stack.enter_context(tc.tile_pool(name="xq", bufs=2))
+        f_pool = stack.enter_context(tc.tile_pool(name="f", bufs=2))
+        soft_pool = stack.enter_context(tc.tile_pool(name="soft", bufs=2))
+        psum_proj = stack.enter_context(tc.psum_pool(name="psum_proj", bufs=HALF_BANKS))
+        psum_flip = stack.enter_context(tc.psum_pool(name="psum_flip", bufs=2))
+        psum_score = stack.enter_context(tc.psum_pool(name="psum_score", bufs=1))
+        stack.enter_context(tc.manual_schedule())
+
+        raw, grouped = {}, {}
+        x_codes, x_scales, proj, f_rows, f_grouped = {}, {}, {}, {}, {}
+        f_codes, f_scales, scores, shift, expd, sums, attn_flipped = {}, {}, {}, {}, {}, {}, {}
+
+        def load_chunk(c):
+            k, h = divmod(c, C_PASSES)
+            n, g = divmod(k, GROUPS)
+            rows = x[n].rearrange("(h p j) t v -> h p j (t v)", h=C_PASSES, p=P, j=PACK)
+            raw[c] = raw_pool.tile([P, PACK, GROUP_COLS], BF16, name="raw")
+            nc.sync.dma_start(
+                out=raw[c][:], in_=rows[h][:, :, g * GROUP_COLS : (g + 1) * GROUP_COLS]
+            )
+
+        def regroup_columns(copy, c, first, last):
+            copy(
+                out=grouped[c][:, first * PACK : last * PACK].rearrange(
+                    "p (c i j) -> p c j i", i=4, j=PACK
+                ),
+                in_=raw[c][:, :, first:last].rearrange("p j (c i) -> p c j i", i=4),
+            )
+
+        def regroup_chunk(c):
+            grouped[c] = grouped_pool.tile(
+                [P, GROUP_COLS * PACK], BF16, name="grouped", align_bytes=64
+            )
+            regroup_columns(nc.vector.tensor_copy, c, 0, VECTOR_COLS)
+            regroup_columns(nc.scalar.copy, c, VECTOR_COLS, GROUP_COLS)
+
+        def quantise_half_chunk(c, half):
+            k, h = divmod(c, C_PASSES)
+            if k not in x_codes:
+                x_codes[k] = xq_pool.tile(
+                    [P, C_PASSES, GROUP_COLS], U32, name="x_codes", align_bytes=64
+                )
+                x_scales[k] = xq_pool.tile(
+                    [P, C_PASSES, GROUP_COLS], U8, name="x_scales", align_bytes=64
+                )
+            cols = slice(half * HALF_COLS, (half + 1) * HALF_COLS)
+            nc.vector.quantize_mx(
+                out=x_codes[k][:, h, cols].bitcast(FP8X4),
+                scales=x_scales[k][:, h, cols],
+                in_=grouped[c][:, half * HALF_COLS * PACK : (half + 1) * HALF_COLS * PACK],
+            )
+
+        def project_bank(k, bank):
+            proj[k, bank] = psum_proj.tile([P, BANK_FRAMES, W_ROWS], F32, name="proj")
+            for f in range(BANK_FRAMES):
+                frame = bank * BANK_FRAMES + f
+                joints = slice(frame * V, (frame + 1) * V)
+                for h in range(C_PASSES):
+                    nc.tensor.matmul_mx(
+                        out=proj[k, bank][:, f, :],
+                        lhsT=x_codes[k][:, h, joints].bitcast(FP8X4),
+                        lhsT_scale=x_scales[k][:, h, joints],
+                        rhs=w_codes[:, h, :].bitcast(FP8X4),
+                        rhs_scale=w_scales[:, h, :],
+                        start=(h == 0),
+                        stop=(h == C_PASSES - 1),
+                    )
+
+        def round_bank(k, bank):
+            if k not in f_rows:
+                f_rows[k] = f_pool.tile(
+                    [P, OPERANDS * MATES * GROUP_FRAMES * PACK], BF16, name="f_rows"
+                )
+            nc.scalar.copy(
+                out=f_rows[k][:].rearrange(
+                    "p (q t j) -> p q t j", q=OPERANDS * MATES, t=GROUP_FRAMES, j=PACK
+                )[:, :, bank * BANK_FRAMES : (bank + 1) * BANK_FRAMES, :],
+                in_=proj[k, bank][:].rearrange("p f (q j) -> p q f j", j=PACK),
+            )
+
+        def flip_group(k):
+            f_words = f_rows[k][:].bitcast(F32)
+            operand_words = MATES * GROUP_FRAMES * 2
+            f_grouped[k] = f_pool.tile(
+                [P, OPERANDS * V * PACK], BF16, name="f_grouped", align_bytes=64
+            )
+            f_grouped_words = f_grouped[k][:].bitcast(F32).rearrange(
+                "p (o v u) -> p o v u", o=OPERANDS, v=V, u=2
+            )
+            for first_operand in range(0, OPERANDS, BANK_OPERANDS):
+                flipped = psum_flip.tile([P, BANK_OPERANDS, 2, V], F32, tag="flipped")
+                for o in range(BANK_OPERANDS):
+                    for u in range(2):
+                        first = (first_operand + o) * operand_words + u
+                        nc.tensor.transpose(
+                            flipped[:, o, u, :],
+                            f_words[:, first : first + operand_words - 1 : 2],
+                            ident[:],
+                        )
+                nc.scalar.copy(
+                    out=f_grouped_words[:, first_operand : first_operand + BANK_OPERANDS],
+                    in_=flipped[:].rearrange("p o u v -> p o v u"),
+                )
+
+        def quantise_group(k):
+            n, g = divmod(k, GROUPS)
+            if n not in f_codes:
+                f_codes[n] = f_pool.tile(
+                    [P, GROUPS, OPERANDS * V], U32, name="f_codes", align_bytes=64
+                )
+                f_scales[n] = f_pool.tile(
+                    [P, GROUPS, OPERANDS * V], U8, name="f_scales", align_bytes=64
+                )
+            nc.vector.quantize_mx(
+                out=f_codes[n][:, g, :].bitcast(FP8X4),
+                scales=f_scales[n][:, g, :],
+                in_=f_grouped[k][:],
+            )
+
+        def score_sample(n):
+            scores[n] = psum_score.tile([P, S, V], F32, name="scores")
+            for s in range(S):
+                fa_cols = slice(s * V, (s + 1) * V)
+                fb_cols = slice((S + s) * V, (S + s + 1) * V)
+                for g in range(GROUPS):
+                    nc.tensor.matmul_mx(
+                        out=scores[n][:, s, :],
+                        lhsT=f_codes[n][:, g, fb_cols].bitcast(FP8X4),
+                        lhsT_scale=f_scales[n][:, g, fb_cols],
+                        rhs=f_codes[n][:, g, fa_cols].bitcast(FP8X4),
+                        rhs_scale=f_scales[n][:, g, fa_cols],
+                        start=(g == 0),
+                        stop=(g == GROUPS - 1),
+                    )
+
+        def softmax_shift(n):
+            top = soft_pool.tile([P, S], F32)
+            nc.vector.tensor_reduce(
+                out=top[:], in_=scores[n][:], axis=mybir.AxisListType.X, op=ALU.max
+            )
+            shift[n] = soft_pool.tile([P, S], F32, name="shift")
+            nc.vector.tensor_scalar(
+                out=shift[n][:], in0=top[:], scalar1=-1.0 / KT, scalar2=None, op0=ALU.mult
+            )
+
+        def softmax_exp(n):
+            expd[n] = soft_pool.tile([P, S, V], F32, name="expd")
+            sums[n] = soft_pool.tile([P, S], F32, name="sums")
+            for s in range(S):
+                nc.scalar.activation(
+                    out=expd[n][:, s, :],
+                    in_=scores[n][:, s, :],
+                    func=ACT.Exp,
+                    bias=shift[n][:, s : s + 1],
+                    scale=1.0 / KT,
+                    accum_out=sums[n][:, s : s + 1],
+                )
+
+        def softmax_divide_and_flip(n):
+            inverse = soft_pool.tile([P, S], F32)
+            nc.vector.reciprocal(out=inverse[:], in_=sums[n][:])
+            attn = soft_pool.tile([P, S, V], F32)
+            nc.vector.tensor_tensor(
+                out=attn[:],
+                in0=expd[n][:],
+                in1=inverse[:].unsqueeze(2).to_broadcast([P, S, V]),
+                op=ALU.mult,
+            )
+            attn_flipped[n] = psum_score.tile([P, S, V], F32, name="attn_flipped")
+            for s in range(S):
+                nc.tensor.transpose(attn_flipped[n][:, s, :], attn[:, s, :], ident[:])
+
+        def add_adjacency_and_store(n):
+            result = soft_pool.tile([P, S, V], F32)
+            nc.vector.tensor_tensor(
+                out=result[:], in0=attn_flipped[n][:], in1=adjacency[:], op=ALU.add
+            )
+            nc.gpsimd.dma_start(out=out[n].rearrange("s v w -> v s w"), in_=result[:])
+
+        ident = consts.tile([P, P], F32)
+        make_identity(nc, ident[:])
+        w_codes, w_scales = quantise_weights(nc, consts, psum_flip, ident, Wa, Wb)
+        for c in range(LOADS_AHEAD):
+            load_chunk(c)
+        a_rows = consts.tile([P, S, V], BF16)
+        pa_rows = consts.tile([P, S, V], BF16)
+        nc.scalar.dma_start(out=a_rows[:], in_=A.rearrange("s v w -> v s w"))
+        nc.scalar.dma_start(out=pa_rows[:], in_=PA.rearrange("s v w -> v s w"))
+        adjacency = consts.tile([P, S, V], F32)
+        nc.gpsimd.tensor_tensor(out=adjacency[:], in0=a_rows[:], in1=pa_rows[:], op=ALU.add)
+
+        for r in range(ALL_GROUPS + 2):
+            first_chunk, second_chunk = C_PASSES * r, C_PASSES * r + 1
+            fresh = r < ALL_GROUPS
+            older = 0 <= r - 1 < ALL_GROUPS
+            sample, scored = divmod(r - 3, GROUPS)
+            soft = r >= 3 and scored == 0
+
+            if first_chunk + LOADS_AHEAD < CHUNKS:
+                load_chunk(first_chunk + LOADS_AHEAD)
+            if fresh:
+                regroup_chunk(first_chunk)
+            if soft:
+                softmax_shift(sample)
+            if older:
+                quantise_half_chunk(first_chunk - 1, 1)
+                for bank in range(HALF_BANKS):
+                    round_bank(r - 1, bank)
+            if soft:
+                softmax_exp(sample)
+            if older:
+                for bank in range(HALF_BANKS, GROUP_BANKS):
+                    project_bank(r - 1, bank)
+                    round_bank(r - 1, bank)
+            if fresh:
+                quantise_half_chunk(first_chunk, 0)
+            if soft:
+                softmax_divide_and_flip(sample)
+            if older:
+                flip_group(r - 1)
+
+            if second_chunk + LOADS_AHEAD < CHUNKS:
+                load_chunk(second_chunk + LOADS_AHEAD)
+            if fresh:
+                regroup_chunk(second_chunk)
+            if soft:
+                add_adjacency_and_store(sample)
+            if fresh:
+                quantise_half_chunk(first_chunk, 1)
+                quantise_half_chunk(second_chunk, 0)
+                for bank in range(HALF_BANKS):
+                    project_bank(r, bank)
+            if older:
+                quantise_group(r - 1)
+                if (r - 1) % GROUPS == GROUPS - 1:
+                    score_sample((r - 1) // GROUPS)

@@ -25,18 +25,13 @@ OPERANDS = SIDES * S
 MATES = INTER // PACK
 
 GROUPS = KT // K_PASS
-ALL_GROUPS = N * GROUPS
 GROUP_FRAMES = T // GROUPS
 GROUP_COLS = GROUP_FRAMES * V
-CHUNKS = ALL_GROUPS * C_PASSES
-HALF_COLS = GROUP_COLS // 2
-SCALAR_COLS = 640
-VECTOR_COLS = GROUP_COLS - SCALAR_COLS
-LOADS_AHEAD = 2
-
+LOAD_COLS = 1024
+LOADS = GROUP_COLS // LOAD_COLS
+PIECE_COLS = 512
+PIECES = LOAD_COLS // PIECE_COLS
 BANK_FRAMES = 2
-GROUP_BANKS = GROUP_FRAMES // BANK_FRAMES
-HALF_BANKS = GROUP_BANKS // 2
 BANK_OPERANDS = 2
 
 FLOPS = 2 * W_ROWS * C * N * T * V + 2 * N * S * V * V * KT
@@ -77,196 +72,32 @@ def quantise_weights(nc, consts, psum_flip, ident, Wa, Wb):
     return w_codes, w_scales
 
 
+def quantise_x_piece(nc, grouped_pool, raw_cols, codes, scales):
+    grouped = grouped_pool.tile([P, PIECE_COLS * PACK], BF16, align_bytes=64)
+    nc.any.tensor_copy(
+        out=grouped[:].rearrange("p (c i j) -> p c j i", i=4, j=PACK),
+        in_=raw_cols.rearrange("p j (c i) -> p c j i", i=4),
+    )
+    nc.vector.quantize_mx(out=codes.bitcast(FP8X4), scales=scales, in_=grouped[:])
+
+
 def tile_unitagcn_pa_t_kernel(tc, x, A, PA, Wa, Wb, out):
     nc = tc.nc
     with ExitStack() as stack:
         consts = stack.enter_context(tc.tile_pool(name="consts", bufs=1))
-        raw_pool = stack.enter_context(tc.tile_pool(name="raw", bufs=LOADS_AHEAD + 1))
-        grouped_pool = stack.enter_context(tc.tile_pool(name="grouped", bufs=3))
-        xq_pool = stack.enter_context(tc.tile_pool(name="xq", bufs=2))
+        raw_pool = stack.enter_context(tc.tile_pool(name="raw", bufs=6))
+        grouped_pool = stack.enter_context(tc.tile_pool(name="grouped", bufs=6))
+        xq_pool = stack.enter_context(tc.tile_pool(name="xq", bufs=3))
         f_pool = stack.enter_context(tc.tile_pool(name="f", bufs=2))
         soft_pool = stack.enter_context(tc.tile_pool(name="soft", bufs=2))
-        psum_proj = stack.enter_context(tc.psum_pool(name="psum_proj", bufs=HALF_BANKS))
+        psum_proj = stack.enter_context(tc.psum_pool(name="psum_proj", bufs=4))
         psum_flip = stack.enter_context(tc.psum_pool(name="psum_flip", bufs=2))
         psum_score = stack.enter_context(tc.psum_pool(name="psum_score", bufs=1))
-        stack.enter_context(tc.manual_schedule())
-
-        raw, grouped = {}, {}
-        x_codes, x_scales, proj, f_rows, f_grouped = {}, {}, {}, {}, {}
-        f_codes, f_scales, scores, shift, expd, sums, attn_flipped = {}, {}, {}, {}, {}, {}, {}
-
-        def load_chunk(c):
-            k, h = divmod(c, C_PASSES)
-            n, g = divmod(k, GROUPS)
-            rows = x[n].rearrange("(h p j) t v -> h p j (t v)", h=C_PASSES, p=P, j=PACK)
-            raw[c] = raw_pool.tile([P, PACK, GROUP_COLS], BF16, name="raw")
-            nc.sync.dma_start(
-                out=raw[c][:], in_=rows[h][:, :, g * GROUP_COLS : (g + 1) * GROUP_COLS]
-            )
-
-        def regroup_columns(copy, c, first, last):
-            copy(
-                out=grouped[c][:, first * PACK : last * PACK].rearrange(
-                    "p (c i j) -> p c j i", i=4, j=PACK
-                ),
-                in_=raw[c][:, :, first:last].rearrange("p j (c i) -> p c j i", i=4),
-            )
-
-        def regroup_chunk(c):
-            grouped[c] = grouped_pool.tile(
-                [P, GROUP_COLS * PACK], BF16, name="grouped", align_bytes=64
-            )
-            regroup_columns(nc.vector.tensor_copy, c, 0, VECTOR_COLS)
-            regroup_columns(nc.scalar.copy, c, VECTOR_COLS, GROUP_COLS)
-
-        def quantise_half_chunk(c, half):
-            k, h = divmod(c, C_PASSES)
-            if k not in x_codes:
-                x_codes[k] = xq_pool.tile(
-                    [P, C_PASSES, GROUP_COLS], U32, name="x_codes", align_bytes=64
-                )
-                x_scales[k] = xq_pool.tile(
-                    [P, C_PASSES, GROUP_COLS], U8, name="x_scales", align_bytes=64
-                )
-            cols = slice(half * HALF_COLS, (half + 1) * HALF_COLS)
-            nc.vector.quantize_mx(
-                out=x_codes[k][:, h, cols].bitcast(FP8X4),
-                scales=x_scales[k][:, h, cols],
-                in_=grouped[c][:, half * HALF_COLS * PACK : (half + 1) * HALF_COLS * PACK],
-            )
-
-        def project_bank(k, bank):
-            proj[k, bank] = psum_proj.tile([P, BANK_FRAMES, W_ROWS], F32, name="proj")
-            for f in range(BANK_FRAMES):
-                frame = bank * BANK_FRAMES + f
-                joints = slice(frame * V, (frame + 1) * V)
-                for h in range(C_PASSES):
-                    nc.tensor.matmul_mx(
-                        out=proj[k, bank][:, f, :],
-                        lhsT=x_codes[k][:, h, joints].bitcast(FP8X4),
-                        lhsT_scale=x_scales[k][:, h, joints],
-                        rhs=w_codes[:, h, :].bitcast(FP8X4),
-                        rhs_scale=w_scales[:, h, :],
-                        start=(h == 0),
-                        stop=(h == C_PASSES - 1),
-                    )
-
-        def round_bank(k, bank):
-            if k not in f_rows:
-                f_rows[k] = f_pool.tile(
-                    [P, OPERANDS * MATES * GROUP_FRAMES * PACK], BF16, name="f_rows"
-                )
-            nc.scalar.copy(
-                out=f_rows[k][:].rearrange(
-                    "p (q t j) -> p q t j", q=OPERANDS * MATES, t=GROUP_FRAMES, j=PACK
-                )[:, :, bank * BANK_FRAMES : (bank + 1) * BANK_FRAMES, :],
-                in_=proj[k, bank][:].rearrange("p f (q j) -> p q f j", j=PACK),
-            )
-
-        def flip_group(k):
-            f_words = f_rows[k][:].bitcast(F32)
-            operand_words = MATES * GROUP_FRAMES * 2
-            f_grouped[k] = f_pool.tile(
-                [P, OPERANDS * V * PACK], BF16, name="f_grouped", align_bytes=64
-            )
-            f_grouped_words = f_grouped[k][:].bitcast(F32).rearrange(
-                "p (o v u) -> p o v u", o=OPERANDS, v=V, u=2
-            )
-            for first_operand in range(0, OPERANDS, BANK_OPERANDS):
-                flipped = psum_flip.tile([P, BANK_OPERANDS, 2, V], F32, tag="flipped")
-                for o in range(BANK_OPERANDS):
-                    for u in range(2):
-                        first = (first_operand + o) * operand_words + u
-                        nc.tensor.transpose(
-                            flipped[:, o, u, :],
-                            f_words[:, first : first + operand_words - 1 : 2],
-                            ident[:],
-                        )
-                nc.scalar.copy(
-                    out=f_grouped_words[:, first_operand : first_operand + BANK_OPERANDS],
-                    in_=flipped[:].rearrange("p o u v -> p o v u"),
-                )
-
-        def quantise_group(k):
-            n, g = divmod(k, GROUPS)
-            if n not in f_codes:
-                f_codes[n] = f_pool.tile(
-                    [P, GROUPS, OPERANDS * V], U32, name="f_codes", align_bytes=64
-                )
-                f_scales[n] = f_pool.tile(
-                    [P, GROUPS, OPERANDS * V], U8, name="f_scales", align_bytes=64
-                )
-            nc.vector.quantize_mx(
-                out=f_codes[n][:, g, :].bitcast(FP8X4),
-                scales=f_scales[n][:, g, :],
-                in_=f_grouped[k][:],
-            )
-
-        def score_sample(n):
-            scores[n] = psum_score.tile([P, S, V], F32, name="scores")
-            for s in range(S):
-                fa_cols = slice(s * V, (s + 1) * V)
-                fb_cols = slice((S + s) * V, (S + s + 1) * V)
-                for g in range(GROUPS):
-                    nc.tensor.matmul_mx(
-                        out=scores[n][:, s, :],
-                        lhsT=f_codes[n][:, g, fb_cols].bitcast(FP8X4),
-                        lhsT_scale=f_scales[n][:, g, fb_cols],
-                        rhs=f_codes[n][:, g, fa_cols].bitcast(FP8X4),
-                        rhs_scale=f_scales[n][:, g, fa_cols],
-                        start=(g == 0),
-                        stop=(g == GROUPS - 1),
-                    )
-
-        def softmax_shift(n):
-            top = soft_pool.tile([P, S], F32)
-            nc.vector.tensor_reduce(
-                out=top[:], in_=scores[n][:], axis=mybir.AxisListType.X, op=ALU.max
-            )
-            shift[n] = soft_pool.tile([P, S], F32, name="shift")
-            nc.vector.tensor_scalar(
-                out=shift[n][:], in0=top[:], scalar1=-1.0 / KT, scalar2=None, op0=ALU.mult
-            )
-
-        def softmax_exp(n):
-            expd[n] = soft_pool.tile([P, S, V], F32, name="expd")
-            sums[n] = soft_pool.tile([P, S], F32, name="sums")
-            for s in range(S):
-                nc.scalar.activation(
-                    out=expd[n][:, s, :],
-                    in_=scores[n][:, s, :],
-                    func=ACT.Exp,
-                    bias=shift[n][:, s : s + 1],
-                    scale=1.0 / KT,
-                    accum_out=sums[n][:, s : s + 1],
-                )
-
-        def softmax_divide_and_flip(n):
-            inverse = soft_pool.tile([P, S], F32)
-            nc.vector.reciprocal(out=inverse[:], in_=sums[n][:])
-            attn = soft_pool.tile([P, S, V], F32)
-            nc.vector.tensor_tensor(
-                out=attn[:],
-                in0=expd[n][:],
-                in1=inverse[:].unsqueeze(2).to_broadcast([P, S, V]),
-                op=ALU.mult,
-            )
-            attn_flipped[n] = psum_score.tile([P, S, V], F32, name="attn_flipped")
-            for s in range(S):
-                nc.tensor.transpose(attn_flipped[n][:, s, :], attn[:, s, :], ident[:])
-
-        def add_adjacency_and_store(n):
-            result = soft_pool.tile([P, S, V], F32)
-            nc.vector.tensor_tensor(
-                out=result[:], in0=attn_flipped[n][:], in1=adjacency[:], op=ALU.add
-            )
-            nc.gpsimd.dma_start(out=out[n].rearrange("s v w -> v s w"), in_=result[:])
 
         ident = consts.tile([P, P], F32)
         make_identity(nc, ident[:])
         w_codes, w_scales = quantise_weights(nc, consts, psum_flip, ident, Wa, Wb)
-        for c in range(LOADS_AHEAD):
-            load_chunk(c)
+
         a_rows = consts.tile([P, S, V], BF16)
         pa_rows = consts.tile([P, S, V], BF16)
         nc.scalar.dma_start(out=a_rows[:], in_=A.rearrange("s v w -> v s w"))
@@ -274,48 +105,128 @@ def tile_unitagcn_pa_t_kernel(tc, x, A, PA, Wa, Wb, out):
         adjacency = consts.tile([P, S, V], F32)
         nc.gpsimd.tensor_tensor(out=adjacency[:], in0=a_rows[:], in1=pa_rows[:], op=ALU.add)
 
-        for r in range(ALL_GROUPS + 2):
-            first_chunk, second_chunk = C_PASSES * r, C_PASSES * r + 1
-            fresh = r < ALL_GROUPS
-            older = 0 <= r - 1 < ALL_GROUPS
-            sample, scored = divmod(r - 3, GROUPS)
-            soft = r >= 3 and scored == 0
+        for n in range(N):
+            x_rows = x[n].rearrange("(h p j) t v -> h p j (t v)", h=C_PASSES, p=P, j=PACK)
+            f_codes = f_pool.tile([P, GROUPS, OPERANDS * V], U32, align_bytes=64)
+            f_scales = f_pool.tile([P, GROUPS, OPERANDS * V], U8, align_bytes=64)
 
-            if first_chunk + LOADS_AHEAD < CHUNKS:
-                load_chunk(first_chunk + LOADS_AHEAD)
-            if fresh:
-                regroup_chunk(first_chunk)
-            if soft:
-                softmax_shift(sample)
-            if older:
-                quantise_half_chunk(first_chunk - 1, 1)
-                for bank in range(HALF_BANKS):
-                    round_bank(r - 1, bank)
-            if soft:
-                softmax_exp(sample)
-            if older:
-                for bank in range(HALF_BANKS, GROUP_BANKS):
-                    project_bank(r - 1, bank)
-                    round_bank(r - 1, bank)
-            if fresh:
-                quantise_half_chunk(first_chunk, 0)
-            if soft:
-                softmax_divide_and_flip(sample)
-            if older:
-                flip_group(r - 1)
+            for g in range(GROUPS):
+                x_codes = xq_pool.tile([P, C_PASSES, GROUP_COLS], U32, align_bytes=64)
+                x_scales = xq_pool.tile([P, C_PASSES, GROUP_COLS], U8, align_bytes=64)
+                for load in range(LOADS):
+                    for h in range(C_PASSES):
+                        first_col = load * LOAD_COLS
+                        raw = raw_pool.tile([P, PACK, LOAD_COLS], BF16)
+                        nc.sync.dma_start(
+                            out=raw[:],
+                            in_=x_rows[h][
+                                :, :, g * GROUP_COLS + first_col : g * GROUP_COLS + first_col + LOAD_COLS
+                            ],
+                        )
+                        for piece in range(PIECES):
+                            cols = slice(
+                                first_col + piece * PIECE_COLS, first_col + (piece + 1) * PIECE_COLS
+                            )
+                            quantise_x_piece(
+                                nc,
+                                grouped_pool,
+                                raw[:, :, piece * PIECE_COLS : (piece + 1) * PIECE_COLS],
+                                x_codes[:, h, cols],
+                                x_scales[:, h, cols],
+                            )
 
-            if second_chunk + LOADS_AHEAD < CHUNKS:
-                load_chunk(second_chunk + LOADS_AHEAD)
-            if fresh:
-                regroup_chunk(second_chunk)
-            if soft:
-                add_adjacency_and_store(sample)
-            if fresh:
-                quantise_half_chunk(first_chunk, 1)
-                quantise_half_chunk(second_chunk, 0)
-                for bank in range(HALF_BANKS):
-                    project_bank(r, bank)
-            if older:
-                quantise_group(r - 1)
-                if (r - 1) % GROUPS == GROUPS - 1:
-                    score_sample((r - 1) // GROUPS)
+                f_rows = f_pool.tile([P, OPERANDS * MATES * GROUP_FRAMES * PACK], BF16)
+                f_rows_view = f_rows[:].rearrange(
+                    "p (q t j) -> p q t j", q=OPERANDS * MATES, t=GROUP_FRAMES, j=PACK
+                )
+                for first_frame in range(0, GROUP_FRAMES, BANK_FRAMES):
+                    proj = psum_proj.tile([P, BANK_FRAMES, W_ROWS], F32)
+                    for f in range(BANK_FRAMES):
+                        joints = slice((first_frame + f) * V, (first_frame + f + 1) * V)
+                        for h in range(C_PASSES):
+                            nc.tensor.matmul_mx(
+                                out=proj[:, f, :],
+                                lhsT=x_codes[:, h, joints].bitcast(FP8X4),
+                                lhsT_scale=x_scales[:, h, joints],
+                                rhs=w_codes[:, h, :].bitcast(FP8X4),
+                                rhs_scale=w_scales[:, h, :],
+                                start=(h == 0),
+                                stop=(h == C_PASSES - 1),
+                            )
+                    nc.scalar.copy(
+                        out=f_rows_view[:, :, first_frame : first_frame + BANK_FRAMES, :],
+                        in_=proj[:].rearrange("p f (q j) -> p q f j", j=PACK),
+                    )
+
+                f_words = f_rows[:].bitcast(F32)
+                operand_words = MATES * GROUP_FRAMES * 2
+                f_grouped = f_pool.tile([P, OPERANDS * V * PACK], BF16, align_bytes=64)
+                f_grouped_words = f_grouped[:].bitcast(F32).rearrange(
+                    "p (o v u) -> p o v u", o=OPERANDS, v=V, u=2
+                )
+                for first_operand in range(0, OPERANDS, BANK_OPERANDS):
+                    flipped = psum_flip.tile([P, BANK_OPERANDS, 2, V], F32, tag="flipped")
+                    for o in range(BANK_OPERANDS):
+                        for u in range(2):
+                            first = (first_operand + o) * operand_words + u
+                            nc.tensor.transpose(
+                                flipped[:, o, u, :],
+                                f_words[:, first : first + operand_words - 1 : 2],
+                                ident[:],
+                            )
+                    nc.scalar.copy(
+                        out=f_grouped_words[:, first_operand : first_operand + BANK_OPERANDS],
+                        in_=flipped[:].rearrange("p o u v -> p o v u"),
+                    )
+                nc.vector.quantize_mx(
+                    out=f_codes[:, g, :].bitcast(FP8X4), scales=f_scales[:, g, :], in_=f_grouped[:]
+                )
+
+            scores = psum_score.tile([P, S, V], F32)
+            for s in range(S):
+                fa_cols = slice(s * V, (s + 1) * V)
+                fb_cols = slice((S + s) * V, (S + s + 1) * V)
+                for g in range(GROUPS):
+                    nc.tensor.matmul_mx(
+                        out=scores[:, s, :],
+                        lhsT=f_codes[:, g, fb_cols].bitcast(FP8X4),
+                        lhsT_scale=f_scales[:, g, fb_cols],
+                        rhs=f_codes[:, g, fa_cols].bitcast(FP8X4),
+                        rhs_scale=f_scales[:, g, fa_cols],
+                        start=(g == 0),
+                        stop=(g == GROUPS - 1),
+                    )
+
+            top = soft_pool.tile([P, S], F32)
+            nc.vector.tensor_reduce(out=top[:], in_=scores[:], axis=mybir.AxisListType.X, op=ALU.max)
+            shift = soft_pool.tile([P, S], F32)
+            nc.vector.tensor_scalar(
+                out=shift[:], in0=top[:], scalar1=-1.0 / KT, scalar2=None, op0=ALU.mult
+            )
+            expd = soft_pool.tile([P, S, V], F32)
+            sums = soft_pool.tile([P, S], F32)
+            for s in range(S):
+                nc.scalar.activation(
+                    out=expd[:, s, :],
+                    in_=scores[:, s, :],
+                    func=ACT.Exp,
+                    bias=shift[:, s : s + 1],
+                    scale=1.0 / KT,
+                    accum_out=sums[:, s : s + 1],
+                )
+            inverse = soft_pool.tile([P, S], F32)
+            nc.vector.reciprocal(out=inverse[:], in_=sums[:])
+            attn = soft_pool.tile([P, S, V], F32)
+            nc.vector.tensor_tensor(
+                out=attn[:],
+                in0=expd[:],
+                in1=inverse[:].unsqueeze(2).to_broadcast([P, S, V]),
+                op=ALU.mult,
+            )
+
+            attn_flipped = psum_score.tile([P, S, V], F32)
+            for s in range(S):
+                nc.tensor.transpose(attn_flipped[:, s, :], attn[:, s, :], ident[:])
+            result = soft_pool.tile([P, S, V], F32)
+            nc.vector.tensor_tensor(out=result[:], in0=attn_flipped[:], in1=adjacency[:], op=ALU.add)
+            nc.gpsimd.dma_start(out=out[n].rearrange("s v w -> v s w"), in_=result[:])

@@ -30,7 +30,10 @@ GROUP_COLS = GROUP_FRAMES * V
 LOAD_COLS = 1024
 LOADS = GROUP_COLS // LOAD_COLS
 PIECE_COLS = 512
-PIECES = LOAD_COLS // PIECE_COLS
+LOAD_PIECES = LOAD_COLS // PIECE_COLS
+GROUP_PIECES = C_PASSES * GROUP_COLS // PIECE_COLS
+SCALAR_PIECES, OF_PIECES = 5, 16
+QUANTISE_LAG = 2
 BANK_FRAMES = 2
 BANK_OPERANDS = 2
 
@@ -39,8 +42,8 @@ FLOPS = 2 * W_ROWS * C * N * T * V + 2 * N * S * V * V * KT
 
 def quantise_weights(nc, consts, psum_flip, ident, Wa, Wb):
     w_rows = consts.tile([P, SIDES * C], BF16)
-    nc.sync.dma_start(out=w_rows[:, 0:C], in_=Wa.rearrange("s i c -> (s i) c"))
-    nc.sync.dma_start(out=w_rows[:, C : 2 * C], in_=Wb.rearrange("s i c -> (s i) c"))
+    nc.scalar.dma_start(out=w_rows[:, 0:C], in_=Wa.rearrange("s i c -> (s i) c"))
+    nc.scalar.dma_start(out=w_rows[:, C : 2 * C], in_=Wb.rearrange("s i c -> (s i) c"))
     w_words = w_rows[:].bitcast(F32)
     pair_words = C // 2
 
@@ -72,13 +75,13 @@ def quantise_weights(nc, consts, psum_flip, ident, Wa, Wb):
     return w_codes, w_scales
 
 
-def quantise_x_piece(nc, grouped_pool, raw_cols, codes, scales):
+def regroup_x_piece(copy, grouped_pool, raw_cols):
     grouped = grouped_pool.tile([P, PIECE_COLS * PACK], BF16, align_bytes=64)
-    nc.any.tensor_copy(
+    copy(
         out=grouped[:].rearrange("p (c i j) -> p c j i", i=4, j=PACK),
         in_=raw_cols.rearrange("p j (c i) -> p c j i", i=4),
     )
-    nc.vector.quantize_mx(out=codes.bitcast(FP8X4), scales=scales, in_=grouped[:])
+    return grouped
 
 
 def tile_unitagcn_pa_t_kernel(tc, x, A, PA, Wa, Wb, out):
@@ -113,6 +116,7 @@ def tile_unitagcn_pa_t_kernel(tc, x, A, PA, Wa, Wb, out):
             for g in range(GROUPS):
                 x_codes = xq_pool.tile([P, C_PASSES, GROUP_COLS], U32, align_bytes=64)
                 x_scales = xq_pool.tile([P, C_PASSES, GROUP_COLS], U8, align_bytes=64)
+                raw_pieces = []
                 for load in range(LOADS):
                     for h in range(C_PASSES):
                         first_col = load * LOAD_COLS
@@ -123,17 +127,35 @@ def tile_unitagcn_pa_t_kernel(tc, x, A, PA, Wa, Wb, out):
                                 :, :, g * GROUP_COLS + first_col : g * GROUP_COLS + first_col + LOAD_COLS
                             ],
                         )
-                        for piece in range(PIECES):
-                            cols = slice(
-                                first_col + piece * PIECE_COLS, first_col + (piece + 1) * PIECE_COLS
+                        for piece in range(LOAD_PIECES):
+                            raw_pieces.append(
+                                (
+                                    raw[:, :, piece * PIECE_COLS : (piece + 1) * PIECE_COLS],
+                                    h,
+                                    slice(
+                                        first_col + piece * PIECE_COLS,
+                                        first_col + (piece + 1) * PIECE_COLS,
+                                    ),
+                                )
                             )
-                            quantise_x_piece(
-                                nc,
+                grouped_pieces = []
+                for i in range(GROUP_PIECES + QUANTISE_LAG):
+                    if i < GROUP_PIECES:
+                        on_scalar = (i * SCALAR_PIECES) % OF_PIECES < SCALAR_PIECES
+                        grouped_pieces.append(
+                            regroup_x_piece(
+                                nc.scalar.copy if on_scalar else nc.vector.tensor_copy,
                                 grouped_pool,
-                                raw[:, :, piece * PIECE_COLS : (piece + 1) * PIECE_COLS],
-                                x_codes[:, h, cols],
-                                x_scales[:, h, cols],
+                                raw_pieces[i][0],
                             )
+                        )
+                    if i >= QUANTISE_LAG:
+                        h, cols = raw_pieces[i - QUANTISE_LAG][1:]
+                        nc.vector.quantize_mx(
+                            out=x_codes[:, h, cols].bitcast(FP8X4),
+                            scales=x_scales[:, h, cols],
+                            in_=grouped_pieces[i - QUANTISE_LAG][:],
+                        )
 
                 f_rows = f_pool.tile([P, OPERANDS * MATES * GROUP_FRAMES * PACK], BF16)
                 f_rows_view = f_rows[:].rearrange(
@@ -229,4 +251,4 @@ def tile_unitagcn_pa_t_kernel(tc, x, A, PA, Wa, Wb, out):
                 nc.tensor.transpose(attn_flipped[:, s, :], attn[:, s, :], ident[:])
             result = soft_pool.tile([P, S, V], F32)
             nc.vector.tensor_tensor(out=result[:], in0=attn_flipped[:], in1=adjacency[:], op=ALU.add)
-            nc.gpsimd.dma_start(out=out[n].rearrange("s v w -> v s w"), in_=result[:])
+            nc.sync.dma_start(out=out[n].rearrange("s v w -> v s w"), in_=result[:])

@@ -27,13 +27,10 @@ MATES = INTER // PACK
 GROUPS = KT // K_PASS
 GROUP_FRAMES = T // GROUPS
 GROUP_COLS = GROUP_FRAMES * V
-LOAD_COLS = 1024
-LOADS = GROUP_COLS // LOAD_COLS
-PIECE_COLS = 512
-LOAD_PIECES = LOAD_COLS // PIECE_COLS
-GROUP_PIECES = C_PASSES * GROUP_COLS // PIECE_COLS
-SCALAR_PIECES, OF_PIECES = 5, 16
-QUANTISE_LAG = 2
+CHUNK_COLS = 1024
+GROUP_CHUNKS = C_PASSES * GROUP_COLS // CHUNK_COLS
+SCALAR_CHUNKS, OF_CHUNKS = 5, 16
+SAMPLES_BEHIND = 1
 BANK_FRAMES = 2
 BANK_OPERANDS = 2
 
@@ -75,11 +72,11 @@ def quantise_weights(nc, consts, psum_flip, ident, Wa, Wb):
     return w_codes, w_scales
 
 
-def regroup_x_piece(copy, grouped_pool, raw_cols):
-    grouped = grouped_pool.tile([P, PIECE_COLS * PACK], BF16, align_bytes=64)
+def regroup_x_chunk(copy, grouped_pool, raw):
+    grouped = grouped_pool.tile([P, CHUNK_COLS * PACK], BF16, align_bytes=64)
     copy(
         out=grouped[:].rearrange("p (c i j) -> p c j i", i=4, j=PACK),
-        in_=raw_cols.rearrange("p j (c i) -> p c j i", i=4),
+        in_=raw[:].rearrange("p j (c i) -> p c j i", i=4),
     )
     return grouped
 
@@ -89,8 +86,11 @@ def tile_unitagcn_pa_t_kernel(tc, x, A, PA, Wa, Wb, out):
     with ExitStack() as stack:
         consts = stack.enter_context(tc.tile_pool(name="consts", bufs=1))
         raw_pool = stack.enter_context(tc.tile_pool(name="raw", bufs=6))
-        grouped_pool = stack.enter_context(tc.tile_pool(name="grouped", bufs=6))
-        xq_pool = stack.enter_context(tc.tile_pool(name="xq", bufs=3))
+        grouped_pool = stack.enter_context(tc.tile_pool(name="grouped", bufs=4))
+        xq_pool = stack.enter_context(tc.tile_pool(name="xq", bufs=2))
+        rows_pool = stack.enter_context(
+            tc.tile_pool(name="rows", bufs=GROUPS * (SAMPLES_BEHIND + 1))
+        )
         f_pool = stack.enter_context(tc.tile_pool(name="f", bufs=2))
         soft_pool = stack.enter_context(tc.tile_pool(name="soft", bufs=2))
         psum_proj = stack.enter_context(tc.psum_pool(name="psum_proj", bufs=4))
@@ -108,101 +108,88 @@ def tile_unitagcn_pa_t_kernel(tc, x, A, PA, Wa, Wb, out):
         adjacency = consts.tile([P, S, V], F32)
         nc.gpsimd.tensor_tensor(out=adjacency[:], in0=a_rows[:], in1=pa_rows[:], op=ALU.add)
 
-        for n in range(N):
+        def project_group(n, g):
             x_rows = x[n].rearrange("(h p j) t v -> h p j (t v)", h=C_PASSES, p=P, j=PACK)
+            x_codes = xq_pool.tile([P, C_PASSES, GROUP_COLS], U32, align_bytes=64)
+            x_scales = xq_pool.tile([P, C_PASSES, GROUP_COLS], U8, align_bytes=64)
+            waiting = None
+            for chunk in range(GROUP_CHUNKS + 1):
+                regrouped = None
+                if chunk < GROUP_CHUNKS:
+                    half, h = divmod(chunk, C_PASSES)
+                    cols = slice(half * CHUNK_COLS, (half + 1) * CHUNK_COLS)
+                    first_col = g * GROUP_COLS + half * CHUNK_COLS
+                    raw = raw_pool.tile([P, PACK, CHUNK_COLS], BF16)
+                    nc.sync.dma_start(
+                        out=raw[:], in_=x_rows[h][:, :, first_col : first_col + CHUNK_COLS]
+                    )
+                    count = 3 + (n * GROUPS + g) * GROUP_CHUNKS + chunk
+                    on_scalar = (count * SCALAR_CHUNKS) % OF_CHUNKS < SCALAR_CHUNKS
+                    regrouped = (
+                        regroup_x_chunk(
+                            nc.scalar.copy if on_scalar else nc.vector.tensor_copy, grouped_pool, raw
+                        ),
+                        x_codes[:, h, cols],
+                        x_scales[:, h, cols],
+                    )
+                if waiting is not None:
+                    nc.vector.quantize_mx(
+                        out=waiting[1].bitcast(FP8X4), scales=waiting[2], in_=waiting[0][:]
+                    )
+                waiting = regrouped
+
+            f_rows = rows_pool.tile([P, OPERANDS * MATES * GROUP_FRAMES * PACK], BF16)
+            f_rows_view = f_rows[:].rearrange(
+                "p (q t j) -> p q t j", q=OPERANDS * MATES, t=GROUP_FRAMES, j=PACK
+            )
+            for first_frame in range(0, GROUP_FRAMES, BANK_FRAMES):
+                proj = psum_proj.tile([P, BANK_FRAMES, W_ROWS], F32)
+                for f in range(BANK_FRAMES):
+                    joints = slice((first_frame + f) * V, (first_frame + f + 1) * V)
+                    for h in range(C_PASSES):
+                        nc.tensor.matmul_mx(
+                            out=proj[:, f, :],
+                            lhsT=x_codes[:, h, joints].bitcast(FP8X4),
+                            lhsT_scale=x_scales[:, h, joints],
+                            rhs=w_codes[:, h, :].bitcast(FP8X4),
+                            rhs_scale=w_scales[:, h, :],
+                            start=(h == 0),
+                            stop=(h == C_PASSES - 1),
+                        )
+                nc.scalar.copy(
+                    out=f_rows_view[:, :, first_frame : first_frame + BANK_FRAMES, :],
+                    in_=proj[:].rearrange("p f (q j) -> p q f j", j=PACK),
+                )
+            return f_rows
+
+        def quantise_group(f_rows, codes, scales):
+            f_words = f_rows[:].bitcast(F32)
+            operand_words = MATES * GROUP_FRAMES * 2
+            f_grouped = f_pool.tile([P, OPERANDS * V * PACK], BF16, align_bytes=64)
+            f_grouped_words = f_grouped[:].bitcast(F32).rearrange(
+                "p (o v u) -> p o v u", o=OPERANDS, v=V, u=2
+            )
+            for first_operand in range(0, OPERANDS, BANK_OPERANDS):
+                flipped = psum_flip.tile([P, BANK_OPERANDS, 2, V], F32, tag="flipped")
+                for o in range(BANK_OPERANDS):
+                    for u in range(2):
+                        first = (first_operand + o) * operand_words + u
+                        nc.tensor.transpose(
+                            flipped[:, o, u, :],
+                            f_words[:, first : first + operand_words - 1 : 2],
+                            ident[:],
+                        )
+                nc.scalar.copy(
+                    out=f_grouped_words[:, first_operand : first_operand + BANK_OPERANDS],
+                    in_=flipped[:].rearrange("p o u v -> p o v u"),
+                )
+            nc.vector.quantize_mx(out=codes.bitcast(FP8X4), scales=scales, in_=f_grouped[:])
+
+        def attend(n, f_rows_of_groups):
             f_codes = f_pool.tile([P, GROUPS, OPERANDS * V], U32, align_bytes=64)
             f_scales = f_pool.tile([P, GROUPS, OPERANDS * V], U8, align_bytes=64)
-
             for g in range(GROUPS):
-                x_codes = xq_pool.tile([P, C_PASSES, GROUP_COLS], U32, align_bytes=64)
-                x_scales = xq_pool.tile([P, C_PASSES, GROUP_COLS], U8, align_bytes=64)
-                raw_pieces = []
-                for load in range(LOADS):
-                    for h in range(C_PASSES):
-                        first_col = load * LOAD_COLS
-                        raw = raw_pool.tile([P, PACK, LOAD_COLS], BF16)
-                        nc.sync.dma_start(
-                            out=raw[:],
-                            in_=x_rows[h][
-                                :, :, g * GROUP_COLS + first_col : g * GROUP_COLS + first_col + LOAD_COLS
-                            ],
-                        )
-                        for piece in range(LOAD_PIECES):
-                            raw_pieces.append(
-                                (
-                                    raw[:, :, piece * PIECE_COLS : (piece + 1) * PIECE_COLS],
-                                    h,
-                                    slice(
-                                        first_col + piece * PIECE_COLS,
-                                        first_col + (piece + 1) * PIECE_COLS,
-                                    ),
-                                )
-                            )
-                grouped_pieces = []
-                for i in range(GROUP_PIECES + QUANTISE_LAG):
-                    if i < GROUP_PIECES:
-                        on_scalar = (i * SCALAR_PIECES) % OF_PIECES < SCALAR_PIECES
-                        grouped_pieces.append(
-                            regroup_x_piece(
-                                nc.scalar.copy if on_scalar else nc.vector.tensor_copy,
-                                grouped_pool,
-                                raw_pieces[i][0],
-                            )
-                        )
-                    if i >= QUANTISE_LAG:
-                        h, cols = raw_pieces[i - QUANTISE_LAG][1:]
-                        nc.vector.quantize_mx(
-                            out=x_codes[:, h, cols].bitcast(FP8X4),
-                            scales=x_scales[:, h, cols],
-                            in_=grouped_pieces[i - QUANTISE_LAG][:],
-                        )
-
-                f_rows = f_pool.tile([P, OPERANDS * MATES * GROUP_FRAMES * PACK], BF16)
-                f_rows_view = f_rows[:].rearrange(
-                    "p (q t j) -> p q t j", q=OPERANDS * MATES, t=GROUP_FRAMES, j=PACK
-                )
-                for first_frame in range(0, GROUP_FRAMES, BANK_FRAMES):
-                    proj = psum_proj.tile([P, BANK_FRAMES, W_ROWS], F32)
-                    for f in range(BANK_FRAMES):
-                        joints = slice((first_frame + f) * V, (first_frame + f + 1) * V)
-                        for h in range(C_PASSES):
-                            nc.tensor.matmul_mx(
-                                out=proj[:, f, :],
-                                lhsT=x_codes[:, h, joints].bitcast(FP8X4),
-                                lhsT_scale=x_scales[:, h, joints],
-                                rhs=w_codes[:, h, :].bitcast(FP8X4),
-                                rhs_scale=w_scales[:, h, :],
-                                start=(h == 0),
-                                stop=(h == C_PASSES - 1),
-                            )
-                    nc.scalar.copy(
-                        out=f_rows_view[:, :, first_frame : first_frame + BANK_FRAMES, :],
-                        in_=proj[:].rearrange("p f (q j) -> p q f j", j=PACK),
-                    )
-
-                f_words = f_rows[:].bitcast(F32)
-                operand_words = MATES * GROUP_FRAMES * 2
-                f_grouped = f_pool.tile([P, OPERANDS * V * PACK], BF16, align_bytes=64)
-                f_grouped_words = f_grouped[:].bitcast(F32).rearrange(
-                    "p (o v u) -> p o v u", o=OPERANDS, v=V, u=2
-                )
-                for first_operand in range(0, OPERANDS, BANK_OPERANDS):
-                    flipped = psum_flip.tile([P, BANK_OPERANDS, 2, V], F32, tag="flipped")
-                    for o in range(BANK_OPERANDS):
-                        for u in range(2):
-                            first = (first_operand + o) * operand_words + u
-                            nc.tensor.transpose(
-                                flipped[:, o, u, :],
-                                f_words[:, first : first + operand_words - 1 : 2],
-                                ident[:],
-                            )
-                    nc.scalar.copy(
-                        out=f_grouped_words[:, first_operand : first_operand + BANK_OPERANDS],
-                        in_=flipped[:].rearrange("p o u v -> p o v u"),
-                    )
-                nc.vector.quantize_mx(
-                    out=f_codes[:, g, :].bitcast(FP8X4), scales=f_scales[:, g, :], in_=f_grouped[:]
-                )
+                quantise_group(f_rows_of_groups[g], f_codes[:, g, :], f_scales[:, g, :])
 
             scores = psum_score.tile([P, S, V], F32)
             for s in range(S):
@@ -252,3 +239,10 @@ def tile_unitagcn_pa_t_kernel(tc, x, A, PA, Wa, Wb, out):
             result = soft_pool.tile([P, S, V], F32)
             nc.vector.tensor_tensor(out=result[:], in0=attn_flipped[:], in1=adjacency[:], op=ALU.add)
             nc.sync.dma_start(out=out[n].rearrange("s v w -> v s w"), in_=result[:])
+
+        projected = {}
+        for n in range(N + SAMPLES_BEHIND):
+            if n < N:
+                projected[n] = [project_group(n, g) for g in range(GROUPS)]
+            if n >= SAMPLES_BEHIND:
+                attend(n - SAMPLES_BEHIND, projected[n - SAMPLES_BEHIND])

from contextlib import ExitStack

import concourse.mybir as mybir
from concourse.masks import make_identity

F32 = mybir.dt.float32
BF16 = mybir.dt.bfloat16
U32 = mybir.dt.uint32
U8 = mybir.dt.uint8
FP8X4 = mybir.dt.float8_e4m3fn_x4
ALU = mybir.AluOpType
ACT = mybir.ActivationFunctionType

N, C, T, V, S, INTER = 4, 1024, 32, 128, 4, 32
KT = INTER * T

P = 128
PACK = 4
K_PASS = P * PACK
C_PASSES = C // K_PASS

SIDES = 2
W_ROWS = SIDES * S * INTER
OPERANDS = SIDES * S
MATES = INTER // PACK

GROUPS = KT // K_PASS
GROUP_FRAMES = T // GROUPS
GROUP_COLS = GROUP_FRAMES * V
CHUNK_COLS = 1024
GROUP_CHUNKS = C_PASSES * GROUP_COLS // CHUNK_COLS
SCALAR_CHUNKS, OF_CHUNKS = 5, 16
SAMPLES_BEHIND = 1
BANK_FRAMES = 2
BANK_OPERANDS = 2

FLOPS = 2 * W_ROWS * C * N * T * V + 2 * N * S * V * V * KT


def quantise_weights(nc, consts, psum_flip, ident, Wa, Wb):
    w_rows = consts.tile([P, SIDES * C], BF16)
    nc.scalar.dma_start(out=w_rows[:, 0:C], in_=Wa.rearrange("s i c -> (s i) c"))
    nc.scalar.dma_start(out=w_rows[:, C : 2 * C], in_=Wb.rearrange("s i c -> (s i) c"))
    w_words = w_rows[:].bitcast(F32)
    pair_words = C // 2

    w_grouped = consts.tile([P, C_PASSES * W_ROWS * PACK], BF16, align_bytes=64)
    w_grouped_words = w_grouped[:].bitcast(F32).rearrange(
        "p (h a q l j u) -> p h a u q l j", h=C_PASSES, a=SIDES, q=S * 2, l=4, j=PACK, u=2
    )
    for h in range(C_PASSES):
        w_flipped = psum_flip.tile([P, SIDES, 2, P], F32, tag="flipped")
        for a in range(SIDES):
            for u in range(2):
                first = a * pair_words + h * (K_PASS // 2) + u
                nc.tensor.transpose(
                    w_flipped[:, a, u, :], w_words[:, first : first + K_PASS // 2 - 1 : 2], ident[:]
                )
        for a in range(SIDES):
            for u in range(2):
                nc.vector.tensor_copy(
                    out=w_grouped_words[:, h, a, u],
                    in_=w_flipped[:, a, u, :].rearrange("p (q j l) -> p q l j", q=S * 2, j=PACK, l=4),
                )
    w_codes = consts.tile([P, C_PASSES, W_ROWS], U32, align_bytes=64)
    w_scales = consts.tile([P, C_PASSES, W_ROWS], U8, align_bytes=64)
    nc.vector.quantize_mx(
        out=w_codes[:].rearrange("p h r -> p (h r)").bitcast(FP8X4),
        scales=w_scales[:].rearrange("p h r -> p (h r)"),
        in_=w_grouped[:],
    )
    return w_codes, w_scales


def regroup_x_chunk(copy, grouped_pool, raw):
    grouped = grouped_pool.tile([P, CHUNK_COLS * PACK], BF16, align_bytes=64)
    copy(
        out=grouped[:].rearrange("p (c i j) -> p c j i", i=4, j=PACK),
        in_=raw[:].rearrange("p j (c i) -> p c j i", i=4),
    )
    return grouped


def tile_unitagcn_pa_t_kernel(tc, x, A, PA, Wa, Wb, out):
    nc = tc.nc
    with ExitStack() as stack:
        consts = stack.enter_context(tc.tile_pool(name="consts", bufs=1))
        raw_pool = stack.enter_context(tc.tile_pool(name="raw", bufs=6))
        grouped_pool = stack.enter_context(tc.tile_pool(name="grouped", bufs=4))
        xq_pool = stack.enter_context(tc.tile_pool(name="xq", bufs=2))
        rows_pool = stack.enter_context(
            tc.tile_pool(name="rows", bufs=GROUPS * (SAMPLES_BEHIND + 1))
        )
        f_pool = stack.enter_context(tc.tile_pool(name="f", bufs=2))
        soft_pool = stack.enter_context(tc.tile_pool(name="soft", bufs=2))
        psum_proj = stack.enter_context(tc.psum_pool(name="psum_proj", bufs=4))
        psum_flip = stack.enter_context(tc.psum_pool(name="psum_flip", bufs=2))
        psum_score = stack.enter_context(tc.psum_pool(name="psum_score", bufs=1))

        ident = consts.tile([P, P], F32)
        make_identity(nc, ident[:])
        w_codes, w_scales = quantise_weights(nc, consts, psum_flip, ident, Wa, Wb)

        a_rows = consts.tile([P, S, V], BF16)
        pa_rows = consts.tile([P, S, V], BF16)
        nc.scalar.dma_start(out=a_rows[:], in_=A.rearrange("s v w -> v s w"))
        nc.scalar.dma_start(out=pa_rows[:], in_=PA.rearrange("s v w -> v s w"))
        adjacency = consts.tile([P, S, V], F32)
        nc.gpsimd.tensor_tensor(out=adjacency[:], in0=a_rows[:], in1=pa_rows[:], op=ALU.add)

        def project_group(n, g):
            x_rows = x[n].rearrange("(h p j) t v -> h p j (t v)", h=C_PASSES, p=P, j=PACK)
            x_codes = xq_pool.tile([P, C_PASSES, GROUP_COLS], U32, align_bytes=64)
            x_scales = xq_pool.tile([P, C_PASSES, GROUP_COLS], U8, align_bytes=64)
            waiting = None
            for chunk in range(GROUP_CHUNKS + 1):
                regrouped = None
                if chunk < GROUP_CHUNKS:
                    half, h = divmod(chunk, C_PASSES)
                    cols = slice(half * CHUNK_COLS, (half + 1) * CHUNK_COLS)
                    first_col = g * GROUP_COLS + half * CHUNK_COLS
                    raw = raw_pool.tile([P, PACK, CHUNK_COLS], BF16)
                    nc.sync.dma_start(
                        out=raw[:], in_=x_rows[h][:, :, first_col : first_col + CHUNK_COLS]
                    )
                    count = 3 + (n * GROUPS + g) * GROUP_CHUNKS + chunk
                    on_scalar = (count * SCALAR_CHUNKS) % OF_CHUNKS < SCALAR_CHUNKS
                    regrouped = (
                        regroup_x_chunk(
                            nc.scalar.copy if on_scalar else nc.vector.tensor_copy, grouped_pool, raw
                        ),
                        x_codes[:, h, cols],
                        x_scales[:, h, cols],
                    )
                if waiting is not None:
                    nc.vector.quantize_mx(
                        out=waiting[1].bitcast(FP8X4), scales=waiting[2], in_=waiting[0][:]
                    )
                waiting = regrouped

            f_rows = rows_pool.tile([P, OPERANDS * MATES * GROUP_FRAMES * PACK], BF16)
            f_rows_view = f_rows[:].rearrange(
                "p (q t j) -> p q t j", q=OPERANDS * MATES, t=GROUP_FRAMES, j=PACK
            )
            for first_frame in range(0, GROUP_FRAMES, BANK_FRAMES):
                proj = psum_proj.tile([P, BANK_FRAMES, W_ROWS], F32)
                for f in range(BANK_FRAMES):
                    joints = slice((first_frame + f) * V, (first_frame + f + 1) * V)
                    for h in range(C_PASSES):
                        nc.tensor.matmul_mx(
                            out=proj[:, f, :],
                            lhsT=x_codes[:, h, joints].bitcast(FP8X4),
                            lhsT_scale=x_scales[:, h, joints],
                            rhs=w_codes[:, h, :].bitcast(FP8X4),
                            rhs_scale=w_scales[:, h, :],
                            start=(h == 0),
                            stop=(h == C_PASSES - 1),
                        )
                nc.scalar.copy(
                    out=f_rows_view[:, :, first_frame : first_frame + BANK_FRAMES, :],
                    in_=proj[:].rearrange("p f (q j) -> p q f j", j=PACK),
                )
            return f_rows

        def quantise_group(f_rows, codes, scales):
            f_words = f_rows[:].bitcast(F32)
            operand_words = MATES * GROUP_FRAMES * 2
            f_grouped = f_pool.tile([P, OPERANDS * V * PACK], BF16, align_bytes=64)
            f_grouped_words = f_grouped[:].bitcast(F32).rearrange(
                "p (o v u) -> p o v u", o=OPERANDS, v=V, u=2
            )
            for first_operand in range(0, OPERANDS, BANK_OPERANDS):
                flipped = psum_flip.tile([P, BANK_OPERANDS, 2, V], F32, tag="flipped")
                for o in range(BANK_OPERANDS):
                    for u in range(2):
                        first = (first_operand + o) * operand_words + u
                        nc.tensor.transpose(
                            flipped[:, o, u, :],
                            f_words[:, first : first + operand_words - 1 : 2],
                            ident[:],
                        )
                nc.scalar.copy(
                    out=f_grouped_words[:, first_operand : first_operand + BANK_OPERANDS],
                    in_=flipped[:].rearrange("p o u v -> p o v u"),
                )
            nc.vector.quantize_mx(out=codes.bitcast(FP8X4), scales=scales, in_=f_grouped[:])

        def attend(n, f_rows_of_groups):
            f_codes = f_pool.tile([P, GROUPS, OPERANDS * V], U32, align_bytes=64)
            f_scales = f_pool.tile([P, GROUPS, OPERANDS * V], U8, align_bytes=64)
            for g in range(GROUPS):
                quantise_group(f_rows_of_groups[g], f_codes[:, g, :], f_scales[:, g, :])

            scores = psum_score.tile([P, S, V], F32)
            for s in range(S):
                fa_cols = slice(s * V, (s + 1) * V)
                fb_cols = slice((S + s) * V, (S + s + 1) * V)
                for g in range(GROUPS):
                    nc.tensor.matmul_mx(
                        out=scores[:, s, :],
                        lhsT=f_codes[:, g, fb_cols].bitcast(FP8X4),
                        lhsT_scale=f_scales[:, g, fb_cols],
                        rhs=f_codes[:, g, fa_cols].bitcast(FP8X4),
                        rhs_scale=f_scales[:, g, fa_cols],
                        start=(g == 0),
                        stop=(g == GROUPS - 1),
                    )

            top = soft_pool.tile([P, S], F32)
            nc.vector.tensor_reduce(out=top[:], in_=scores[:], axis=mybir.AxisListType.X, op=ALU.max)
            shift = soft_pool.tile([P, S], F32)
            nc.vector.tensor_scalar(
                out=shift[:], in0=top[:], scalar1=-1.0 / KT, scalar2=None, op0=ALU.mult
            )
            expd = soft_pool.tile([P, S, V], F32)
            sums = soft_pool.tile([P, S], F32)
            for s in range(S):
                nc.scalar.activation(
                    out=expd[:, s, :],
                    in_=scores[:, s, :],
                    func=ACT.Exp,
                    bias=shift[:, s : s + 1],
                    scale=1.0 / KT,
                    accum_out=sums[:, s : s + 1],
                )
            inverse = soft_pool.tile([P, S], F32)
            nc.vector.reciprocal(out=inverse[:], in_=sums[:])
            attn = soft_pool.tile([P, S, V], F32)
            nc.vector.tensor_tensor(
                out=attn[:],
                in0=expd[:],
                in1=inverse[:].unsqueeze(2).to_broadcast([P, S, V]),
                op=ALU.mult,
            )

            attn_flipped = psum_score.tile([P, S, V], F32)
            for s in range(S):
                nc.tensor.transpose(attn_flipped[:, s, :], attn[:, s, :], ident[:])
            result = soft_pool.tile([P, S, V], F32)
            nc.vector.tensor_tensor(out=result[:], in0=attn_flipped[:], in1=adjacency[:], op=ALU.add)
            nc.sync.dma_start(out=out[n].rearrange("s v w -> v s w"), in_=result[:])

        projected = {}
        for n in range(N + SAMPLES_BEHIND):
            if n < N:
                projected[n] = [project_group(n, g) for g in range(GROUPS)]
            if n >= SAMPLES_BEHIND:
                attend(n - SAMPLES_BEHIND, projected[n - SAMPLES_BEHIND])
